import numpy as np
import ml_dtypes

BF16 = ml_dtypes.bfloat16


def bf(x):
    return np.asarray(x, np.float32).astype(BF16)


def f32(x):
    return np.asarray(x, np.float32)


def f64(x):
    return np.asarray(x).astype(np.float64)


def striped(idx):
    return np.tile(idx.reshape(-1, 16).T, (8, 1))


R, A, C, S, N = 128, 2, 512, 4096, 2048
BASE = 10000.0


def sincos_table():
    inv_freq = 1.0 / BASE ** (np.arange(R) / R)
    ang = f32(np.einsum('i,j->ij', np.arange(S), inv_freq))
    return np.ascontiguousarray(np.concatenate([np.sin(ang), np.cos(ang)], axis=-1).T)


def setup_inputs():
    return {'table': f32(sincos_table()), 't': f32(np.random.standard_normal((C, N))), 'offs': striped(np.random.permutation(np.tile(np.arange(S), 2))[:N])}


def reference(table, t, offs):
    idx = offs[:16].T.reshape(-1)
    picked = f64(table)[:, idx]
    sin, cos = picked[:R], picked[R:]
    tt = f64(t).reshape(A, -1, R, N)
    ev, od = tt[:, 0], tt[:, 1]
    return np.stack([cos * ev - sin * od, cos * od + sin * ev], axis=1).reshape(C, N)

@@ -1,0 +1,70 @@
+import concourse.mybir as mybir
+
+F32 = mybir.dt.float32
+U16 = mybir.dt.uint16
+MULT = mybir.AluOpType.mult
+ADD = mybir.AluOpType.add
+SUBTRACT = mybir.AluOpType.subtract
+
+P = 128
+POSITIONS = 4096
+TOKENS = 2048
+HEADS = 2
+PIECE = 512
+PIECES = TOKENS // PIECE
+
+
+def token_columns(piece):
+    return slice(piece * PIECE, (piece + 1) * PIECE)
+
+
+def block_rows(block):
+    return slice(block * P, (block + 1) * P)
+
+
+def looked_up(window, offsets, piece):
+    return window[:].indirect(offsets[:, piece * PIECE // 16 : (piece + 1) * PIECE // 16])
+
+
+def tile_flaxgptjattention_kernel(tc, table, t, offs, out):
+    nc = tc.nc
+    with (
+        tc.tile_pool(name="held", bufs=1) as held,
+        tc.tile_pool(name="ring", bufs=4) as ring,
+    ):
+        offsets = held.tile([P, TOKENS // 16], U16, name="offsets")
+        nc.sync.dma_start(offsets[:], offs)
+        cos = held.tile([P, POSITIONS], F32, name="cos")
+        nc.sync.dma_start(cos[:], table[P : 2 * P, :])
+        sin = held.tile([P, POSITIONS], F32, name="sin")
+        features = [held.tile([P, TOKENS], F32, name=f"features{block}") for block in range(2 * HEADS)]
+        for head in range(HEADS):
+            for piece in range(PIECES):
+                for block in (2 * head, 2 * head + 1):
+                    nc.sync.dma_start(
+                        features[block][:, token_columns(piece)], t[block_rows(block), token_columns(piece)]
+                    )
+            if head == 0:
+                nc.sync.dma_start(sin[:], table[0:P, :])
+
+        for head in range(HEADS):
+            first, second = features[2 * head], features[2 * head + 1]
+            turned_first = held.tile([P, TOKENS], F32, name=f"turned_first{head}")
+            turned_second = held.tile([P, TOKENS], F32, name=f"turned_second{head}")
+
+            for piece in range(PIECES):
+                cols = token_columns(piece)
+                nc.vector.tensor_tensor(turned_first[:, cols], looked_up(cos, offsets, piece), first[:, cols], MULT)
+                nc.vector.tensor_tensor(turned_second[:, cols], looked_up(cos, offsets, piece), second[:, cols], MULT)
+
+            for piece in range(PIECES):
+                cols = token_columns(piece)
+                sin_second = ring.tile([P, PIECE], F32, name="sin_second")
+                nc.vector.tensor_tensor(sin_second[:], looked_up(sin, offsets, piece), second[:, cols], MULT)
+                nc.vector.tensor_tensor(turned_first[:, cols], turned_first[:, cols], sin_second[:], SUBTRACT)
+                nc.scalar.dma_start(out[block_rows(2 * head), cols], turned_first[:, cols])
+
+                sin_first = ring.tile([P, PIECE], F32, name="sin_first")
+                nc.vector.tensor_tensor(sin_first[:], looked_up(sin, offsets, piece), first[:, cols], MULT)
+                nc.vector.tensor_tensor(turned_second[:, cols], turned_second[:, cols], sin_first[:], ADD)
+                nc.scalar.dma_start(out[block_rows(2 * head + 1), cols], turned_second[:, cols])

@@ -1,10 +1,9 @@
 import concourse.mybir as mybir
+from concourse.masks import make_identity
 
 F32 = mybir.dt.float32
 U16 = mybir.dt.uint16
 MULT = mybir.AluOpType.mult
-ADD = mybir.AluOpType.add
-SUBTRACT = mybir.AluOpType.subtract
 
 P = 128
 POSITIONS = 4096
@@ -12,6 +11,7 @@ TOKENS = 2048
 HEADS = 2
 PIECE = 512
 PIECES = TOKENS // PIECE
+BANKS = 8
 
 
 def token_columns(piece):
@@ -30,7 +30,9 @@ def tile_flaxgptjattention_kernel(tc, table, t, offs, out):
     nc = tc.nc
     with (
         tc.tile_pool(name="held", bufs=1) as held,
-        tc.tile_pool(name="ring", bufs=4) as ring,
+        tc.tile_pool(name="products", bufs=6) as products,
+        tc.tile_pool(name="staging", bufs=4) as staging,
+        tc.psum_pool(name="sums", bufs=BANKS) as sums,
     ):
         offsets = held.tile([P, TOKENS // 16], U16, name="offsets")
         nc.sync.dma_start(offsets[:], offs)
@@ -47,24 +49,35 @@ def tile_flaxgptjattention_kernel(tc, table, t, offs, out):
             if head == 0:
                 nc.sync.dma_start(sin[:], table[0:P, :])
 
+        plus = held.tile([P, P], F32, name="plus")
+        make_identity(nc, plus[:])
+        minus = held.tile([P, P], F32, name="minus")
+        nc.scalar.mul(minus[:], plus[:], -1.0)
+
         for head in range(HEADS):
             first, second = features[2 * head], features[2 * head + 1]
-            turned_first = held.tile([P, TOKENS], F32, name=f"turned_first{head}")
-            turned_second = held.tile([P, TOKENS], F32, name=f"turned_second{head}")
+
+            first_sums, second_sums = [], []
+            for piece in range(PIECES):
+                for feature, opened in ((first, first_sums), (second, second_sums)):
+                    product = products.tile([P, PIECE], F32, name="product")
+                    nc.vector.tensor_tensor(
+                        product[:], looked_up(cos, offsets, piece), feature[:, token_columns(piece)], MULT
+                    )
+                    bank = sums.tile([P, PIECE], F32, name="bank")
+                    nc.tensor.matmul(bank[:], plus[:], product[:], start=True, stop=False)
+                    opened.append(bank)
 
             for piece in range(PIECES):
-                cols = token_columns(piece)
-                nc.vector.tensor_tensor(turned_first[:, cols], looked_up(cos, offsets, piece), first[:, cols], MULT)
-                nc.vector.tensor_tensor(turned_second[:, cols], looked_up(cos, offsets, piece), second[:, cols], MULT)
-
-            for piece in range(PIECES):
-                cols = token_columns(piece)
-                sin_second = ring.tile([P, PIECE], F32, name="sin_second")
-                nc.vector.tensor_tensor(sin_second[:], looked_up(sin, offsets, piece), second[:, cols], MULT)
-                nc.vector.tensor_tensor(turned_first[:, cols], turned_first[:, cols], sin_second[:], SUBTRACT)
-                nc.scalar.dma_start(out[block_rows(2 * head), cols], turned_first[:, cols])
-
-                sin_first = ring.tile([P, PIECE], F32, name="sin_first")
-                nc.vector.tensor_tensor(sin_first[:], looked_up(sin, offsets, piece), first[:, cols], MULT)
-                nc.vector.tensor_tensor(turned_second[:, cols], turned_second[:, cols], sin_first[:], ADD)
-                nc.scalar.dma_start(out[block_rows(2 * head + 1), cols], turned_second[:, cols])
+                for feature, sign, bank, block in (
+                    (second, minus, first_sums[piece], 2 * head),
+                    (first, plus, second_sums[piece], 2 * head + 1),
+                ):
+                    product = products.tile([P, PIECE], F32, name="product")
+                    nc.vector.tensor_tensor(
+                        product[:], looked_up(sin, offsets, piece), feature[:, token_columns(piece)], MULT
+                    )
+                    nc.tensor.matmul(bank[:], sign[:], product[:], start=False, stop=True)
+                    turned = staging.tile([P, PIECE], F32, name="turned")
+                    nc.scalar.copy(turned[:], bank[:])
+                    nc.sync.dma_start(out[block_rows(block), token_columns(piece)], turned[:])

@@ -4,6 +4,8 @@ from concourse.masks import make_identity
 F32 = mybir.dt.float32
 U16 = mybir.dt.uint16
 MULT = mybir.AluOpType.mult
+ADD = mybir.AluOpType.add
+SUBTRACT = mybir.AluOpType.subtract
 
 P = 128
 POSITIONS = 4096
@@ -12,6 +14,7 @@ HEADS = 2
 PIECE = 512
 PIECES = TOKENS // PIECE
 BANKS = 8
+ADDED_ON_VECTOR = (HEADS - 1, PIECES - 1)
 
 
 def token_columns(piece):
@@ -22,8 +25,11 @@ def block_rows(block):
     return slice(block * P, (block + 1) * P)
 
 
-def looked_up(window, offsets, piece):
-    return window[:].indirect(offsets[:, piece * PIECE // 16 : (piece + 1) * PIECE // 16])
+def gathered_product(nc, pool, window, offsets, feature, piece):
+    product = pool.tile([P, PIECE], F32, name="product")
+    picked = window[:].indirect(offsets[:, piece * PIECE // 16 : (piece + 1) * PIECE // 16])
+    nc.vector.tensor_tensor(product[:], picked, feature[:, token_columns(piece)], MULT)
+    return product
 
 
 def tile_flaxgptjattention_kernel(tc, table, t, offs, out):
@@ -31,6 +37,7 @@ def tile_flaxgptjattention_kernel(tc, table, t, offs, out):
     with (
         tc.tile_pool(name="held", bufs=1) as held,
         tc.tile_pool(name="products", bufs=6) as products,
+        tc.tile_pool(name="kept", bufs=2) as kept,
         tc.tile_pool(name="staging", bufs=4) as staging,
         tc.psum_pool(name="sums", bufs=BANKS) as sums,
     ):
@@ -60,24 +67,24 @@ def tile_flaxgptjattention_kernel(tc, table, t, offs, out):
             first_sums, second_sums = [], []
             for piece in range(PIECES):
                 for feature, opened in ((first, first_sums), (second, second_sums)):
-                    product = products.tile([P, PIECE], F32, name="product")
-                    nc.vector.tensor_tensor(
-                        product[:], looked_up(cos, offsets, piece), feature[:, token_columns(piece)], MULT
-                    )
-                    bank = sums.tile([P, PIECE], F32, name="bank")
-                    nc.tensor.matmul(bank[:], plus[:], product[:], start=True, stop=False)
-                    opened.append(bank)
+                    if (head, piece) == ADDED_ON_VECTOR:
+                        opened.append(gathered_product(nc, kept, cos, offsets, feature, piece))
+                    else:
+                        product = gathered_product(nc, products, cos, offsets, feature, piece)
+                        bank = sums.tile([P, PIECE], F32, name="bank")
+                        nc.tensor.matmul(bank[:], plus[:], product[:], start=True, stop=False)
+                        opened.append(bank)
 
             for piece in range(PIECES):
-                for feature, sign, bank, block in (
-                    (second, minus, first_sums[piece], 2 * head),
-                    (first, plus, second_sums[piece], 2 * head + 1),
+                for feature, sign, op, opened, block in (
+                    (second, minus, SUBTRACT, first_sums[piece], 2 * head),
+                    (first, plus, ADD, second_sums[piece], 2 * head + 1),
                 ):
-                    product = products.tile([P, PIECE], F32, name="product")
-                    nc.vector.tensor_tensor(
-                        product[:], looked_up(sin, offsets, piece), feature[:, token_columns(piece)], MULT
-                    )
-                    nc.tensor.matmul(bank[:], sign[:], product[:], start=False, stop=True)
+                    product = gathered_product(nc, products, sin, offsets, feature, piece)
                     turned = staging.tile([P, PIECE], F32, name="turned")
-                    nc.scalar.copy(turned[:], bank[:])
+                    if (head, piece) == ADDED_ON_VECTOR:
+                        nc.vector.tensor_tensor(turned[:], opened[:], product[:], op)
+                    else:
+                        nc.tensor.matmul(opened[:], sign[:], product[:], start=False, stop=True)
+                        nc.scalar.copy(turned[:], opened[:])
                     nc.sync.dma_start(out[block_rows(block), token_columns(piece)], turned[:])

@@ -11,24 +11,30 @@ P = 128
 POSITIONS = 4096
 TOKENS = 2048
 HEADS = 2
-PIECE = 512
-PIECES = TOKENS // PIECE
+BANK = 512
 BANKS = 8
-ADDED_ON_VECTOR = (HEADS - 1, PIECES - 1)
+SHORT = BANK
 
-
-def token_columns(piece):
-    return slice(piece * PIECE, (piece + 1) * PIECE)
+SUMMED_ON_TENSOR = (
+    (slice(0, SHORT), slice(SHORT, TOKENS)),
+    (slice(0, TOKENS - SHORT),),
+)
+SUMMED_ON_VECTOR = slice(TOKENS - SHORT, TOKENS)
 
 
 def block_rows(block):
     return slice(block * P, (block + 1) * P)
 
 
-def gathered_product(nc, pool, window, offsets, feature, piece):
-    product = pool.tile([P, PIECE], F32, name="product")
-    picked = window[:].indirect(offsets[:, piece * PIECE // 16 : (piece + 1) * PIECE // 16])
-    nc.vector.tensor_tensor(product[:], picked, feature[:, token_columns(piece)], MULT)
+def bank_starts(span):
+    return range(span.start, span.stop, BANK)
+
+
+def gathered_product(nc, pool, window, offsets, feature, span):
+    width = span.stop - span.start
+    product = pool.tile([P, width], F32, name=f"product{width}")
+    picked = window[:].indirect(offsets[:, span.start // 16 : span.stop // 16])
+    nc.vector.tensor_tensor(product[:], picked, feature[:, span], MULT)
     return product
 
 
@@ -36,8 +42,7 @@ def tile_flaxgptjattention_kernel(tc, table, t, offs, out):
     nc = tc.nc
     with (
         tc.tile_pool(name="held", bufs=1) as held,
-        tc.tile_pool(name="products", bufs=6) as products,
-        tc.tile_pool(name="kept", bufs=2) as kept,
+        tc.tile_pool(name="products", bufs=3) as products,
         tc.tile_pool(name="staging", bufs=4) as staging,
         tc.psum_pool(name="sums", bufs=BANKS) as sums,
     ):
@@ -47,14 +52,12 @@ def tile_flaxgptjattention_kernel(tc, table, t, offs, out):
         nc.sync.dma_start(cos[:], table[P : 2 * P, :])
         sin = held.tile([P, POSITIONS], F32, name="sin")
         features = [held.tile([P, TOKENS], F32, name=f"features{block}") for block in range(2 * HEADS)]
-        for head in range(HEADS):
-            for piece in range(PIECES):
-                for block in (2 * head, 2 * head + 1):
-                    nc.sync.dma_start(
-                        features[block][:, token_columns(piece)], t[block_rows(block), token_columns(piece)]
-                    )
-            if head == 0:
-                nc.sync.dma_start(sin[:], table[0:P, :])
+        for span in SUMMED_ON_TENSOR[0]:
+            for block in (0, 1):
+                nc.sync.dma_start(features[block][:, span], t[block_rows(block), span])
+        nc.sync.dma_start(sin[:], table[0:P, :])
+        for block in (2, 3):
+            nc.sync.dma_start(features[block][:], t[block_rows(block), :])
 
         plus = held.tile([P, P], F32, name="plus")
         make_identity(nc, plus[:])
@@ -64,27 +67,34 @@ def tile_flaxgptjattention_kernel(tc, table, t, offs, out):
         for head in range(HEADS):
             first, second = features[2 * head], features[2 * head + 1]
 
-            first_sums, second_sums = [], []
-            for piece in range(PIECES):
-                for feature, opened in ((first, first_sums), (second, second_sums)):
-                    if (head, piece) == ADDED_ON_VECTOR:
-                        opened.append(gathered_product(nc, kept, cos, offsets, feature, piece))
-                    else:
-                        product = gathered_product(nc, products, cos, offsets, feature, piece)
-                        bank = sums.tile([P, PIECE], F32, name="bank")
-                        nc.tensor.matmul(bank[:], plus[:], product[:], start=True, stop=False)
-                        opened.append(bank)
+            opened = {}
+            for span in SUMMED_ON_TENSOR[head]:
+                for feature, block in ((first, 2 * head), (second, 2 * head + 1)):
+                    product = gathered_product(nc, products, cos, offsets, feature, span)
+                    for start in bank_starts(span):
+                        bank = sums.tile([P, BANK], F32, name="bank")
+                        part = product[:, start - span.start : start - span.start + BANK]
+                        nc.tensor.matmul(bank[:], plus[:], part, start=True, stop=False)
+                        opened[(block, start)] = bank
 
-            for piece in range(PIECES):
-                for feature, sign, op, opened, block in (
-                    (second, minus, SUBTRACT, first_sums[piece], 2 * head),
-                    (first, plus, ADD, second_sums[piece], 2 * head + 1),
-                ):
-                    product = gathered_product(nc, products, sin, offsets, feature, piece)
-                    turned = staging.tile([P, PIECE], F32, name="turned")
-                    if (head, piece) == ADDED_ON_VECTOR:
-                        nc.vector.tensor_tensor(turned[:], opened[:], product[:], op)
-                    else:
-                        nc.tensor.matmul(opened[:], sign[:], product[:], start=False, stop=True)
-                        nc.scalar.copy(turned[:], opened[:])
-                    nc.sync.dma_start(out[block_rows(block), token_columns(piece)], turned[:])
+            for span in SUMMED_ON_TENSOR[head]:
+                for feature, sign, block in ((second, minus, 2 * head), (first, plus, 2 * head + 1)):
+                    product = gathered_product(nc, products, sin, offsets, feature, span)
+                    for start in bank_starts(span):
+                        bank = opened[(block, start)]
+                        part = product[:, start - span.start : start - span.start + BANK]
+                        nc.tensor.matmul(bank[:], sign[:], part, start=False, stop=True)
+                        turned = staging.tile([P, BANK], F32, name="turned")
+                        nc.scalar.copy(turned[:], bank[:])
+                        nc.sync.dma_start(out[block_rows(block), start : start + BANK], turned[:])
+
+        span = SUMMED_ON_VECTOR
+        for with_cos, with_sin, op, block in (
+            (first, second, SUBTRACT, 2 * HEADS - 2),
+            (second, first, ADD, 2 * HEADS - 1),
+        ):
+            cos_product = gathered_product(nc, products, cos, offsets, with_cos, span)
+            sin_product = gathered_product(nc, products, sin, offsets, with_sin, span)
+            turned = staging.tile([P, BANK], F32, name="turned")
+            nc.vector.tensor_tensor(turned[:], cos_product[:], sin_product[:], op)
+            nc.sync.dma_start(out[block_rows(block), span], turned[:])

@@ -42,8 +42,8 @@ def tile_flaxgptjattention_kernel(tc, table, t, offs, out):
     nc = tc.nc
     with (
         tc.tile_pool(name="held", bufs=1) as held,
-        tc.tile_pool(name="products", bufs=3) as products,
-        tc.tile_pool(name="staging", bufs=4) as staging,
+        tc.tile_pool(name="products", bufs=6) as products,
+        tc.tile_pool(name="staging", bufs=8) as staging,
         tc.psum_pool(name="sums", bufs=BANKS) as sums,
     ):
         offsets = held.tile([P, TOKENS // 16], U16, name="offsets")

@@ -13,37 +13,36 @@ TOKENS = 2048
 HEADS = 2
 BANK = 512
 BANKS = 8
-SHORT = BANK
 
-SUMMED_ON_TENSOR = (
-    (slice(0, SHORT), slice(SHORT, TOKENS)),
-    (slice(0, TOKENS - SHORT),),
+COS_STAGES = (
+    ((slice(0, 128), slice(128, 512)), (slice(512, TOKENS),)),
+    ((slice(0, 1024),), (slice(1024, 1792),)),
 )
-SUMMED_ON_VECTOR = slice(TOKENS - SHORT, TOKENS)
+SIN_STAGES = (
+    ((slice(0, 1024),), (slice(1024, TOKENS),)),
+    ((slice(0, 1024),), (slice(1024, 1792),)),
+)
+SUMMED_ON_VECTOR = slice(1792, TOKENS)
 
 
 def block_rows(block):
     return slice(block * P, (block + 1) * P)
 
 
-def bank_starts(span):
-    return range(span.start, span.stop, BANK)
+def banks_of(stage):
+    stop = stage[-1].stop
+    return [slice(start, min(start + BANK, stop)) for start in range(stage[0].start, stop, BANK)]
 
 
-def gathered_product(nc, pool, window, offsets, feature, span):
-    width = span.stop - span.start
-    product = pool.tile([P, width], F32, name=f"product{width}")
+def gather_and_multiply(nc, product, window, offsets, feature, span):
     picked = window[:].indirect(offsets[:, span.start // 16 : span.stop // 16])
-    nc.vector.tensor_tensor(product[:], picked, feature[:, span], MULT)
-    return product
+    nc.vector.tensor_tensor(product[:, span], picked, feature[:, span], MULT)
 
 
 def tile_flaxgptjattention_kernel(tc, table, t, offs, out):
     nc = tc.nc
     with (
         tc.tile_pool(name="held", bufs=1) as held,
-        tc.tile_pool(name="products", bufs=6) as products,
-        tc.tile_pool(name="staging", bufs=8) as staging,
         tc.psum_pool(name="sums", bufs=BANKS) as sums,
     ):
         offsets = held.tile([P, TOKENS // 16], U16, name="offsets")
@@ -52,12 +51,17 @@ def tile_flaxgptjattention_kernel(tc, table, t, offs, out):
         nc.sync.dma_start(cos[:], table[P : 2 * P, :])
         sin = held.tile([P, POSITIONS], F32, name="sin")
         features = [held.tile([P, TOKENS], F32, name=f"features{block}") for block in range(2 * HEADS)]
-        for span in SUMMED_ON_TENSOR[0]:
-            for block in (0, 1):
-                nc.sync.dma_start(features[block][:, span], t[block_rows(block), span])
+        for stage in COS_STAGES[0]:
+            for span in stage:
+                for block in (0, 1):
+                    nc.sync.dma_start(features[block][:, span], t[block_rows(block), span])
         nc.sync.dma_start(sin[:], table[0:P, :])
         for block in (2, 3):
             nc.sync.dma_start(features[block][:], t[block_rows(block), :])
+
+        cos_products = [held.tile([P, TOKENS], F32, name=f"cos_product{block}") for block in range(2 * HEADS)]
+        sin_products = [held.tile([P, TOKENS], F32, name=f"sin_product{block}") for block in range(2 * HEADS)]
+        turned = [held.tile([P, TOKENS], F32, name=f"turned{block}") for block in range(2 * HEADS)]
 
         plus = held.tile([P, P], F32, name="plus")
         make_identity(nc, plus[:])
@@ -65,36 +69,37 @@ def tile_flaxgptjattention_kernel(tc, table, t, offs, out):
         nc.scalar.mul(minus[:], plus[:], -1.0)
 
         for head in range(HEADS):
-            first, second = features[2 * head], features[2 * head + 1]
+            first, second = 2 * head, 2 * head + 1
 
             opened = {}
-            for span in SUMMED_ON_TENSOR[head]:
-                for feature, block in ((first, 2 * head), (second, 2 * head + 1)):
-                    product = gathered_product(nc, products, cos, offsets, feature, span)
-                    for start in bank_starts(span):
+            for stage in COS_STAGES[head]:
+                for span in stage:
+                    for block in (first, second):
+                        gather_and_multiply(nc, cos_products[block], cos, offsets, features[block], span)
+                for block in (first, second):
+                    for columns in banks_of(stage):
                         bank = sums.tile([P, BANK], F32, name="bank")
-                        part = product[:, start - span.start : start - span.start + BANK]
-                        nc.tensor.matmul(bank[:], plus[:], part, start=True, stop=False)
-                        opened[(block, start)] = bank
+                        opened[(block, columns.start)] = bank[:, : columns.stop - columns.start]
+                        nc.tensor.matmul(
+                            opened[(block, columns.start)], plus[:], cos_products[block][:, columns], start=True, stop=False
+                        )
 
-            for span in SUMMED_ON_TENSOR[head]:
-                for feature, sign, block in ((second, minus, 2 * head), (first, plus, 2 * head + 1)):
-                    product = gathered_product(nc, products, sin, offsets, feature, span)
-                    for start in bank_starts(span):
-                        bank = opened[(block, start)]
-                        part = product[:, start - span.start : start - span.start + BANK]
-                        nc.tensor.matmul(bank[:], sign[:], part, start=False, stop=True)
-                        turned = staging.tile([P, BANK], F32, name="turned")
-                        nc.scalar.copy(turned[:], bank[:])
-                        nc.sync.dma_start(out[block_rows(block), start : start + BANK], turned[:])
+            for stage in SIN_STAGES[head]:
+                for span in stage:
+                    for other in (second, first):
+                        gather_and_multiply(nc, sin_products[other], sin, offsets, features[other], span)
+                for block, other, sign in ((first, second, minus), (second, first, plus)):
+                    for columns in banks_of(stage):
+                        total = opened[(block, columns.start)]
+                        nc.tensor.matmul(total, sign[:], sin_products[other][:, columns], start=False, stop=True)
+                        nc.scalar.copy(turned[block][:, columns], total)
+                        if columns.stop % BANK == 0:
+                            nc.sync.dma_start(out[block_rows(block), columns], turned[block][:, columns])
 
         span = SUMMED_ON_VECTOR
-        for with_cos, with_sin, op, block in (
-            (first, second, SUBTRACT, 2 * HEADS - 2),
-            (second, first, ADD, 2 * HEADS - 1),
-        ):
-            cos_product = gathered_product(nc, products, cos, offsets, with_cos, span)
-            sin_product = gathered_product(nc, products, sin, offsets, with_sin, span)
-            turned = staging.tile([P, BANK], F32, name="turned")
-            nc.vector.tensor_tensor(turned[:], cos_product[:], sin_product[:], op)
-            nc.sync.dma_start(out[block_rows(block), span], turned[:])
+        last_bank = slice(TOKENS - BANK, TOKENS)
+        for block, other, op in ((first, second, SUBTRACT), (second, first, ADD)):
+            gather_and_multiply(nc, cos_products[block], cos, offsets, features[block], span)
+            gather_and_multiply(nc, sin_products[other], sin, offsets, features[other], span)
+            nc.vector.tensor_tensor(turned[block][:, span], cos_products[block][:, span], sin_products[other][:, span], op)
+            nc.sync.dma_start(out[block_rows(block), last_bank], turned[block][:, last_bank])

@@ -48,7 +48,8 @@ def tile_flaxgptjattention_kernel(tc, table, t, offs, out):
         offsets = held.tile([P, TOKENS // 16], U16, name="offsets")
         nc.sync.dma_start(offsets[:], offs)
         cos = held.tile([P, POSITIONS], F32, name="cos")
-        nc.sync.dma_start(cos[:], table[P : 2 * P, :])
+        nc.sync.dma_start(cos[:, : POSITIONS // 2], table[P : 2 * P, : POSITIONS // 2])
+        nc.scalar.dma_start(cos[:, POSITIONS // 2 :], table[P : 2 * P, POSITIONS // 2 :])
         sin = held.tile([P, POSITIONS], F32, name="sin")
         features = [held.tile([P, TOKENS], F32, name=f"features{block}") for block in range(2 * HEADS)]
         for stage in COS_STAGES[0]:

@@ -14,15 +14,24 @@ HEADS = 2
 BANK = 512
 BANKS = 8
 
-COS_STAGES = (
-    ((slice(0, 128), slice(128, 512)), (slice(512, TOKENS),)),
-    ((slice(0, 1024),), (slice(1024, 1792),)),
-)
-SIN_STAGES = (
-    ((slice(0, 1024),), (slice(1024, TOKENS),)),
-    ((slice(0, 1024),), (slice(1024, 1792),)),
+COS, SIN = "cos", "sin"
+STAGES = (
+    (
+        (COS, (slice(0, 128), slice(128, 512))),
+        (COS, (slice(512, TOKENS),)),
+        (SIN, (slice(0, 1024),)),
+        (SIN, (slice(1024, TOKENS),)),
+    ),
+    (
+        (COS, (slice(0, 1024),)),
+        (SIN, (slice(0, 1024),)),
+        (COS, (slice(1024, 1792),)),
+        (SIN, (slice(1024, 1536),)),
+        (SIN, (slice(1536, 1792),)),
+    ),
 )
 SUMMED_ON_VECTOR = slice(1792, TOKENS)
+LINK = 8
 
 
 def block_rows(block):
@@ -52,10 +61,11 @@ def tile_flaxgptjattention_kernel(tc, table, t, offs, out):
         nc.scalar.dma_start(cos[:, POSITIONS // 2 :], table[P : 2 * P, POSITIONS // 2 :])
         sin = held.tile([P, POSITIONS], F32, name="sin")
         features = [held.tile([P, TOKENS], F32, name=f"features{block}") for block in range(2 * HEADS)]
-        for stage in COS_STAGES[0]:
-            for span in stage:
-                for block in (0, 1):
-                    nc.sync.dma_start(features[block][:, span], t[block_rows(block), span])
+        for window, stage in STAGES[0]:
+            if window == COS:
+                for span in stage:
+                    for block in (0, 1):
+                        nc.sync.dma_start(features[block][:, span], t[block_rows(block), span])
         nc.sync.dma_start(sin[:], table[0:P, :])
         for block in (2, 3):
             nc.sync.dma_start(features[block][:], t[block_rows(block), :])
@@ -73,34 +83,37 @@ def tile_flaxgptjattention_kernel(tc, table, t, offs, out):
             first, second = 2 * head, 2 * head + 1
 
             opened = {}
-            for stage in COS_STAGES[head]:
-                for span in stage:
+            for window, stage in STAGES[head]:
+                if window == COS:
+                    for span in stage:
+                        for block in (first, second):
+                            gather_and_multiply(nc, cos_products[block], cos, offsets, features[block], span)
                     for block in (first, second):
-                        gather_and_multiply(nc, cos_products[block], cos, offsets, features[block], span)
-                for block in (first, second):
-                    for columns in banks_of(stage):
-                        bank = sums.tile([P, BANK], F32, name="bank")
-                        opened[(block, columns.start)] = bank[:, : columns.stop - columns.start]
-                        nc.tensor.matmul(
-                            opened[(block, columns.start)], plus[:], cos_products[block][:, columns], start=True, stop=False
-                        )
-
-            for stage in SIN_STAGES[head]:
-                for span in stage:
-                    for other in (second, first):
-                        gather_and_multiply(nc, sin_products[other], sin, offsets, features[other], span)
-                for block, other, sign in ((first, second, minus), (second, first, plus)):
-                    for columns in banks_of(stage):
-                        total = opened[(block, columns.start)]
-                        nc.tensor.matmul(total, sign[:], sin_products[other][:, columns], start=False, stop=True)
-                        nc.scalar.copy(turned[block][:, columns], total)
-                        if columns.stop % BANK == 0:
+                        for columns in banks_of(stage):
+                            bank = sums.tile([P, BANK], F32, name="bank")
+                            opened[(block, columns.start)] = bank[:, : columns.stop - columns.start]
+                            nc.tensor.matmul(
+                                opened[(block, columns.start)], plus[:], cos_products[block][:, columns], start=True, stop=False
+                            )
+                else:
+                    for span in stage:
+                        for other in (second, first):
+                            gather_and_multiply(nc, sin_products[other], sin, offsets, features[other], span)
+                    for block, other, sign in ((first, second, minus), (second, first, plus)):
+                        for columns in banks_of(stage):
+                            total = opened[(block, columns.start)]
+                            nc.tensor.matmul(total, sign[:], sin_products[other][:, columns], start=False, stop=True)
+                            nc.scalar.copy(turned[block][:, columns], total)
+                            if columns.stop == SUMMED_ON_VECTOR.start:
+                                columns = slice(columns.start, columns.stop - LINK)
                             nc.sync.dma_start(out[block_rows(block), columns], turned[block][:, columns])
 
         span = SUMMED_ON_VECTOR
-        last_bank = slice(TOKENS - BANK, TOKENS)
-        for block, other, op in ((first, second, SUBTRACT), (second, first, ADD)):
+        linked = slice(span.start - LINK, span.stop)
+        for block in (first, second):
             gather_and_multiply(nc, cos_products[block], cos, offsets, features[block], span)
+        for other in (second, first):
             gather_and_multiply(nc, sin_products[other], sin, offsets, features[other], span)
+        for block, other, op in ((first, second, SUBTRACT), (second, first, ADD)):
             nc.vector.tensor_tensor(turned[block][:, span], cos_products[block][:, span], sin_products[other][:, span], op)
-            nc.sync.dma_start(out[block_rows(block), last_bank], turned[block][:, last_bank])
+            nc.sync.dma_start(out[block_rows(block), linked], turned[block][:, linked])

@@ -18,7 +18,8 @@ COS, SIN = "cos", "sin"
 STAGES = (
     (
         (COS, (slice(0, 128), slice(128, 512))),
-        (COS, (slice(512, TOKENS),)),
+        (COS, (slice(512, 1024),)),
+        (COS, (slice(1024, TOKENS),)),
         (SIN, (slice(0, 1024),)),
         (SIN, (slice(1024, TOKENS),)),
     ),

import concourse.mybir as mybir
from concourse.masks import make_identity

F32 = mybir.dt.float32
U16 = mybir.dt.uint16
MULT = mybir.AluOpType.mult
ADD = mybir.AluOpType.add
SUBTRACT = mybir.AluOpType.subtract

P = 128
POSITIONS = 4096
TOKENS = 2048
HEADS = 2
BANK = 512
BANKS = 8

COS, SIN = "cos", "sin"
STAGES = (
    (
        (COS, (slice(0, 128), slice(128, 512))),
        (COS, (slice(512, 1024),)),
        (COS, (slice(1024, TOKENS),)),
        (SIN, (slice(0, 1024),)),
        (SIN, (slice(1024, TOKENS),)),
    ),
    (
        (COS, (slice(0, 1024),)),
        (SIN, (slice(0, 1024),)),
        (COS, (slice(1024, 1792),)),
        (SIN, (slice(1024, 1536),)),
        (SIN, (slice(1536, 1792),)),
    ),
)
SUMMED_ON_VECTOR = slice(1792, TOKENS)
LINK = 8


def block_rows(block):
    return slice(block * P, (block + 1) * P)


def banks_of(stage):
    stop = stage[-1].stop
    return [slice(start, min(start + BANK, stop)) for start in range(stage[0].start, stop, BANK)]


def gather_and_multiply(nc, product, window, offsets, feature, span):
    picked = window[:].indirect(offsets[:, span.start // 16 : span.stop // 16])
    nc.vector.tensor_tensor(product[:, span], picked, feature[:, span], MULT)


def tile_flaxgptjattention_kernel(tc, table, t, offs, out):
    nc = tc.nc
    with (
        tc.tile_pool(name="held", bufs=1) as held,
        tc.psum_pool(name="sums", bufs=BANKS) as sums,
    ):
        offsets = held.tile([P, TOKENS // 16], U16, name="offsets")
        nc.sync.dma_start(offsets[:], offs)
        cos = held.tile([P, POSITIONS], F32, name="cos")
        nc.sync.dma_start(cos[:, : POSITIONS // 2], table[P : 2 * P, : POSITIONS // 2])
        nc.scalar.dma_start(cos[:, POSITIONS // 2 :], table[P : 2 * P, POSITIONS // 2 :])
        sin = held.tile([P, POSITIONS], F32, name="sin")
        features = [held.tile([P, TOKENS], F32, name=f"features{block}") for block in range(2 * HEADS)]
        for window, stage in STAGES[0]:
            if window == COS:
                for span in stage:
                    for block in (0, 1):
                        nc.sync.dma_start(features[block][:, span], t[block_rows(block), span])
        nc.sync.dma_start(sin[:], table[0:P, :])
        for block in (2, 3):
            nc.sync.dma_start(features[block][:], t[block_rows(block), :])

        cos_products = [held.tile([P, TOKENS], F32, name=f"cos_product{block}") for block in range(2 * HEADS)]
        sin_products = [held.tile([P, TOKENS], F32, name=f"sin_product{block}") for block in range(2 * HEADS)]
        turned = [held.tile([P, TOKENS], F32, name=f"turned{block}") for block in range(2 * HEADS)]

        plus = held.tile([P, P], F32, name="plus")
        make_identity(nc, plus[:])
        minus = held.tile([P, P], F32, name="minus")
        nc.scalar.mul(minus[:], plus[:], -1.0)

        for head in range(HEADS):
            first, second = 2 * head, 2 * head + 1

            opened = {}
            for window, stage in STAGES[head]:
                if window == COS:
                    for span in stage:
                        for block in (first, second):
                            gather_and_multiply(nc, cos_products[block], cos, offsets, features[block], span)
                    for block in (first, second):
                        for columns in banks_of(stage):
                            bank = sums.tile([P, BANK], F32, name="bank")
                            opened[(block, columns.start)] = bank[:, : columns.stop - columns.start]
                            nc.tensor.matmul(
                                opened[(block, columns.start)], plus[:], cos_products[block][:, columns], start=True, stop=False
                            )
                else:
                    for span in stage:
                        for other in (second, first):
                            gather_and_multiply(nc, sin_products[other], sin, offsets, features[other], span)
                    for block, other, sign in ((first, second, minus), (second, first, plus)):
                        for columns in banks_of(stage):
                            total = opened[(block, columns.start)]
                            nc.tensor.matmul(total, sign[:], sin_products[other][:, columns], start=False, stop=True)
                            nc.scalar.copy(turned[block][:, columns], total)
                            if columns.stop == SUMMED_ON_VECTOR.start:
                                columns = slice(columns.start, columns.stop - LINK)
                            nc.sync.dma_start(out[block_rows(block), columns], turned[block][:, columns])

        span = SUMMED_ON_VECTOR
        linked = slice(span.start - LINK, span.stop)
        for block in (first, second):
            gather_and_multiply(nc, cos_products[block], cos, offsets, features[block], span)
        for other in (second, first):
            gather_and_multiply(nc, sin_products[other], sin, offsets, features[other], span)
        for block, other, op in ((first, second, SUBTRACT), (second, first, ADD)):
            nc.vector.tensor_tensor(turned[block][:, span], cos_products[block][:, span], sin_products[other][:, span], op)
            nc.sync.dma_start(out[block_rows(block), linked], turned[block][:, linked])
